import numpy as np
import ml_dtypes


def mxq(x, axis, fmt="e4m3"):
    dtype, down = {"e4m3": (ml_dtypes.float8_e4m3fn, 7), "e5m2": (ml_dtypes.float8_e5m2, 14)}[fmt]
    v = np.moveaxis(np.asarray(x, np.float32).astype(ml_dtypes.bfloat16).astype(np.float64), axis, -1)
    blocks = v.reshape(v.shape[:-1] + (-1, 32))
    amax = np.abs(blocks).max(-1, keepdims=True)
    byte = np.maximum(np.where(amax > 0, np.frexp(amax)[1] - 1 + 127, 0) - down, 1)
    scale = np.exp2(byte - 127.0)
    codes = (blocks / scale).astype(np.float32).astype(dtype).astype(np.float64)
    return np.moveaxis((codes * scale).reshape(v.shape), -1, axis)


WIDE = False


def mx_kscale(k):
    if not WIDE:
        return np.ones(k)
    levels = np.array([10, -10, 5, -5, 0])
    a = np.random.permutation(np.resize(levels, k // 512 * 4)).reshape(k // 512, 4)
    idx = np.arange(k)
    return np.exp2(a[idx // 512, idx % 128 // 32])


BF16 = ml_dtypes.bfloat16


def bf(x):
    return np.asarray(x, np.float32).astype(BF16)


def f64(x):
    return np.asarray(x).astype(np.float64)


B, I0, I1, I2, O0, O1, O2, R1, R2 = 256, 128, 8, 4, 1, 1, 128, 128, 128


def pos(lo, *shape):
    return np.random.uniform(lo, 2.0 - lo, shape)


def setup_inputs():
    a1 = mx_kscale(R1 * I1)[::I1]
    a2 = mx_kscale(R2 * I2)[::I2]
    return {"vector": bf(pos(0.25, B, I0, I1, I2) * pos(0.5, B, 1, I1, I2) * pos(0.5, B, 1, 1, 1)),
            "core0": bf(pos(0.25, 1, O0, I0, R1) * pos(0.5, 1, O0, 1, 1) * pos(0.5, 1, 1, 1, R1) / I0 * a1),
            "core1": bf(pos(0.25, R1, O1, I1, R2) * pos(0.5, 1, O1, 1, 1) * pos(0.5, 1, 1, 1, R2) / (R1 * I1) / a1[:, None, None, None] * a2),
            "core2": bf(pos(0.25, R2, O2, I2, 1) * pos(0.5, 1, O2, 1, 1) / (R2 * I2) / a2[:, None, None, None])}


def _contract(res, bs, core, quantised):
    r, o, i, k = core.shape
    rem = res.shape[3:]
    a = res.reshape(bs, r * i, -1)
    x = a.shape[2]
    a = a.transpose(0, 2, 1).reshape(bs * x, r * i)
    w = core.transpose(0, 2, 1, 3).reshape(r * i, o * k)
    if quantised:
        y = mxq(a, 1, "e4m3") @ mxq(w, 0, "e4m3")
    else:
        y = a @ w
    y = y.reshape(bs, x, o, k).transpose(0, 2, 3, 1)
    return y.reshape(bs * o, k, *rem), bs * o


def reference(vector, core0, core1, core2):
    bs0 = vector.shape[0]
    res = f64(vector)[:, None]
    bs = bs0
    res, bs = _contract(res, bs, f64(core0), False)
    res, bs = _contract(res, bs, f64(core1), True)
    res, bs = _contract(res, bs, f64(core2), True)
    res = np.squeeze(res, axis=-1)
    return res.reshape(bs0, core0.shape[1], core1.shape[1], core2.shape[1])

@@ -1,0 +1,182 @@
+from contextlib import ExitStack
+
+import concourse.mybir as mybir
+from concourse.masks import make_identity
+
+F32 = mybir.dt.float32
+BF16 = mybir.dt.bfloat16
+U32 = mybir.dt.uint32
+U8 = mybir.dt.uint8
+FP8X4 = mybir.dt.float8_e4m3fn_x4
+
+P = 128
+PACK = 4
+BANK = 512
+
+B, I0, I1, I2 = 256, 128, 8, 4
+R1, R2, O2 = 128, 128, 128
+
+B_TILES = B // P
+PASSES = I1 // PACK
+PAIRS = I2 // 2
+WORDS = I1 * PAIRS
+COLS = P * I2
+BANK_COLS = BANK // PACK
+BANKS = COLS // BANK_COLS
+HALF = COLS // 2
+
+RUN = 4
+RUNS = 4
+GROUPS = 8
+
+FLOPS = 2 * B * I1 * I2 * I0 * R1 + 2 * B * I2 * R1 * I1 * R2 + 2 * B * R2 * I2 * O2
+
+
+def ranks_by_partition(ap):
+    return ap.rearrange("k (g n v) -> k n g v", g=GROUPS, n=RUNS, v=RUN)
+
+
+def partitions_split(ap):
+    return ap.rearrange("k (n g v) -> k n g v", g=GROUPS, n=RUNS, v=RUN)
+
+
+def tile_ttmatrix_s_kernel(tc, vector, core0, core1, core2, out):
+    nc = tc.nc
+    units = [(bt, c) for bt in range(B_TILES) for c in range(PASSES)]
+
+    with ExitStack() as ctx:
+        keep = ctx.enter_context(tc.tile_pool(name="keep", bufs=1))
+        xt_banks = ctx.enter_context(tc.psum_pool(name="xt_banks", bufs=2))
+        h0_banks = ctx.enter_context(tc.psum_pool(name="h0_banks", bufs=4))
+        h1_banks = ctx.enter_context(tc.psum_pool(name="h1_banks", bufs=1))
+        out_banks = ctx.enter_context(tc.psum_pool(name="out_banks", bufs=1))
+
+        x_rows = vector.rearrange("b i j k -> b (i j k)")
+        x_sb = [keep.tile([P, I0 * I1 * I2], BF16, name="x_sb%d" % bt) for bt in range(B_TILES)]
+        core0_sb = keep.tile([I0, R1], BF16)
+        core1_sb = keep.tile([R1, I1 * R2], BF16)
+        core2_sb = keep.tile([R2, O2 * I2], BF16, align_bytes=64)
+        nc.sync.dma_start(out=x_sb[0][:], in_=x_rows[0:P, :])
+        nc.sync.dma_start(out=core0_sb[:], in_=core0.rearrange("a o i r -> (a o i) r"))
+        nc.sync.dma_start(out=core1_sb[:], in_=core1.rearrange("r o i k -> r (o i k)"))
+        nc.sync.dma_start(out=x_sb[1][:], in_=x_rows[P : 2 * P, :])
+        nc.sync.dma_start(out=core2_sb[:], in_=core2.rearrange("r o i x -> r (o i x)"))
+
+        ident = keep.tile([P, P], F32)
+        make_identity(nc, ident[:])
+        rank_select = keep.tile([R1, P], BF16)
+        nc.vector.tensor_copy(out=partitions_split(rank_select[:]), in_=ranks_by_partition(ident[:]))
+
+        xT = [keep.tile([I0, PACK * P * PAIRS], F32, name="xT%d" % u) for u in range(len(units))]
+        h0_bf = [
+            keep.tile([P, COLS, PACK], BF16, name="h0_bf%d" % u, align_bytes=64)
+            for u in range(len(units))
+        ]
+        h0_codes = [
+            keep.tile([P, COLS], U32, name="h0_codes%d" % u, align_bytes=64)
+            for u in range(len(units))
+        ]
+        h0_scales = [
+            keep.tile([P, COLS], U8, name="h0_scales%d" % u, align_bytes=64)
+            for u in range(len(units))
+        ]
+
+        def transpose_words(u, s):
+            bt, c = units[u]
+            x_words = x_sb[bt][:].bitcast(F32).rearrange("b (i w) -> b w i", w=WORDS)
+            xt = xt_banks.tile([I0, 2 * PAIRS, P], F32)
+            first_word = (PACK * c + 2 * s) * PAIRS
+            for slot in range(2 * PAIRS):
+                nc.tensor.transpose(xt[:, slot, :], x_words[:, first_word + slot, :], ident[:])
+            xT_words = xT[u][:].rearrange("i (j b h) -> i j b h", j=PACK, h=PAIRS)
+            nc.vector.tensor_copy(
+                out=xT_words[:, 2 * s : 2 * s + 2, :, :],
+                in_=xt[:].rearrange("i (j h) b -> i j b h", h=PAIRS),
+            )
+
+        def first_contraction(u, q):
+            cols = slice(q * BANK_COLS, (q + 1) * BANK_COLS)
+            x_cols = xT[u][:].bitcast(BF16).rearrange("i (j w) -> i j w", j=PACK)
+            h0 = h0_banks.tile([P, PACK, BANK_COLS], F32, tag="h0")
+            nc.tensor.matmul(out=h0[:], lhsT=core0_p[:], rhs=x_cols[:, :, cols], start=True, stop=True)
+            nc.scalar.copy(out=h0_bf[u][:, cols, :], in_=h0[:].rearrange("p j w -> p w j"))
+
+        def quantise_h0(u, half):
+            cols = slice(half * HALF, (half + 1) * HALF)
+            nc.vector.quantize_mx(
+                out=h0_codes[u][:, cols].bitcast(FP8X4),
+                scales=h0_scales[u][:, cols],
+                in_=h0_bf[u][:, cols, :].rearrange("p w j -> p (w j)"),
+            )
+
+        def second_and_third_contraction(bt):
+            h1 = h1_banks.tile([R2, COLS], F32)
+            for c in range(PASSES):
+                u = units.index((bt, c))
+                nc.tensor.matmul_mx(
+                    out=h1[:],
+                    lhsT=w1_codes[:, c, :].bitcast(FP8X4),
+                    lhsT_scale=w1_scales[:, c, :],
+                    rhs=h0_codes[u][:].bitcast(FP8X4),
+                    rhs_scale=h0_scales[u][:],
+                    start=(c == 0),
+                    stop=(c == PASSES - 1),
+                )
+            h1_bf = keep.tile([R2, COLS], BF16, name="h1_bf%d" % bt, align_bytes=64)
+            h1_codes = keep.tile([R2, P], U32, name="h1_codes%d" % bt, align_bytes=64)
+            h1_scales = keep.tile([R2, P], U8, name="h1_scales%d" % bt, align_bytes=64)
+            nc.scalar.copy(out=h1_bf[:], in_=h1[:])
+            nc.vector.quantize_mx(out=h1_codes[:].bitcast(FP8X4), scales=h1_scales[:], in_=h1_bf[:])
+
+            acc = out_banks.tile([P, O2], F32)
+            nc.tensor.matmul_mx(
+                out=acc[:],
+                lhsT=h1_codes[:].bitcast(FP8X4),
+                lhsT_scale=h1_scales[:],
+                rhs=w2_codes[:].bitcast(FP8X4),
+                rhs_scale=w2_scales[:],
+                start=True,
+                stop=True,
+            )
+            out_sb = keep.tile([P, O2], F32, name="out_sb%d" % bt)
+            nc.vector.tensor_copy(out=out_sb[:], in_=acc[:])
+            nc.sync.dma_start(
+                out=out.rearrange("b x y o -> b (x y o)")[bt * P : (bt + 1) * P, :], in_=out_sb[:]
+            )
+
+        transpose_words(0, 0)
+        transpose_words(0, 1)
+
+        core0_p = keep.tile([I0, P], BF16)
+        nc.vector.tensor_copy(out=partitions_split(core0_p[:]), in_=ranks_by_partition(core0_sb[:]))
+
+        w1_bf = keep.tile([P, PASSES, R2, PACK], BF16, align_bytes=64)
+        w1_codes = keep.tile([P, PASSES, R2], U32, align_bytes=64)
+        w1_scales = keep.tile([P, PASSES, R2], U8, align_bytes=64)
+        core1_passes = core1_sb[:].rearrange("r (c j k) -> r c j k", c=PASSES, j=PACK)
+        for c in range(PASSES):
+            w1_rows = h0_banks.tile([P, PACK, R2], F32, tag="h0")
+            nc.tensor.matmul(
+                out=w1_rows[:], lhsT=rank_select[:], rhs=core1_passes[:, c, :, :], start=True, stop=True
+            )
+            nc.scalar.copy(out=w1_bf[:, c, :, :], in_=w1_rows[:].rearrange("p j k -> p k j"))
+        nc.vector.quantize_mx(
+            out=w1_codes[:].rearrange("p c k -> p (c k)").bitcast(FP8X4),
+            scales=w1_scales[:].rearrange("p c k -> p (c k)"),
+            in_=w1_bf[:].rearrange("p c k j -> p (c k j)"),
+        )
+
+        w2_codes = keep.tile([R2, O2], U32, align_bytes=64)
+        w2_scales = keep.tile([R2, O2], U8, align_bytes=64)
+        nc.vector.quantize_mx(out=w2_codes[:].bitcast(FP8X4), scales=w2_scales[:], in_=core2_sb[:])
+
+        for u in range(len(units)):
+            for half in range(2):
+                for q in range(half * BANKS // 2, (half + 1) * BANKS // 2):
+                    first_contraction(u, q)
+                if u + 1 < len(units):
+                    transpose_words(u + 1, half)
+                quantise_h0(u, half)
+            bt, c = units[u]
+            if c == PASSES - 1:
+                second_and_third_contraction(bt)

@@ -22,8 +22,9 @@ PAIRS = I2 // 2
 WORDS = I1 * PAIRS
 COLS = P * I2
 BANK_COLS = BANK // PACK
-BANKS = COLS // BANK_COLS
 HALF = COLS // 2
+UNITS = B_TILES * PASSES
+AHEAD = 2
 
 RUN = 4
 RUNS = 4
@@ -42,7 +43,6 @@ def partitions_split(ap):
 
 def tile_ttmatrix_s_kernel(tc, vector, core0, core1, core2, out):
     nc = tc.nc
-    units = [(bt, c) for bt in range(B_TILES) for c in range(PASSES)]
 
     with ExitStack() as ctx:
         keep = ctx.enter_context(tc.tile_pool(name="keep", bufs=1))
@@ -51,47 +51,54 @@ def tile_ttmatrix_s_kernel(tc, vector, core0, core1, core2, out):
         h1_banks = ctx.enter_context(tc.psum_pool(name="h1_banks", bufs=1))
         out_banks = ctx.enter_context(tc.psum_pool(name="out_banks", bufs=1))
 
+        ctx.enter_context(tc.manual_schedule())
+
         x_rows = vector.rearrange("b i j k -> b (i j k)")
         x_sb = [keep.tile([P, I0 * I1 * I2], BF16, name="x_sb%d" % bt) for bt in range(B_TILES)]
         core0_sb = keep.tile([I0, R1], BF16)
         core1_sb = keep.tile([R1, I1 * R2], BF16)
         core2_sb = keep.tile([R2, O2 * I2], BF16, align_bytes=64)
-        nc.sync.dma_start(out=x_sb[0][:], in_=x_rows[0:P, :])
         nc.sync.dma_start(out=core0_sb[:], in_=core0.rearrange("a o i r -> (a o i) r"))
         nc.sync.dma_start(out=core1_sb[:], in_=core1.rearrange("r o i k -> r (o i k)"))
-        nc.sync.dma_start(out=x_sb[1][:], in_=x_rows[P : 2 * P, :])
+        for bt in range(B_TILES):
+            nc.sync.dma_start(out=x_sb[bt][:], in_=x_rows[bt * P : (bt + 1) * P, :])
         nc.sync.dma_start(out=core2_sb[:], in_=core2.rearrange("r o i x -> r (o i x)"))
 
-        ident = keep.tile([P, P], F32)
-        make_identity(nc, ident[:])
-        rank_select = keep.tile([R1, P], BF16)
-        nc.vector.tensor_copy(out=partitions_split(rank_select[:]), in_=ranks_by_partition(ident[:]))
-
-        xT = [keep.tile([I0, PACK * P * PAIRS], F32, name="xT%d" % u) for u in range(len(units))]
+        xT = [keep.tile([I0, PACK * P * PAIRS], F32, name="xT%d" % u) for u in range(UNITS)]
         h0_bf = [
-            keep.tile([P, COLS, PACK], BF16, name="h0_bf%d" % u, align_bytes=64)
-            for u in range(len(units))
+            keep.tile([P, COLS, PACK], BF16, name="h0_bf%d" % u, align_bytes=64) for u in range(UNITS)
         ]
         h0_codes = [
-            keep.tile([P, COLS], U32, name="h0_codes%d" % u, align_bytes=64)
-            for u in range(len(units))
+            keep.tile([P, COLS], U32, name="h0_codes%d" % u, align_bytes=64) for u in range(UNITS)
         ]
         h0_scales = [
-            keep.tile([P, COLS], U8, name="h0_scales%d" % u, align_bytes=64)
-            for u in range(len(units))
+            keep.tile([P, COLS], U8, name="h0_scales%d" % u, align_bytes=64) for u in range(UNITS)
+        ]
+        h1_codes = [
+            keep.tile([R2, P], U32, name="h1_codes%d" % bt, align_bytes=64) for bt in range(B_TILES)
+        ]
+        h1_scales = [
+            keep.tile([R2, P], U8, name="h1_scales%d" % bt, align_bytes=64) for bt in range(B_TILES)
         ]
 
+        def empty_bank(by_vector, out_ap, bank_ap):
+            if by_vector:
+                nc.vector.tensor_copy(out=out_ap, in_=bank_ap)
+            else:
+                nc.scalar.copy(out=out_ap, in_=bank_ap)
+
         def transpose_words(u, s):
-            bt, c = units[u]
+            bt, c = divmod(u, PASSES)
             x_words = x_sb[bt][:].bitcast(F32).rearrange("b (i w) -> b w i", w=WORDS)
             xt = xt_banks.tile([I0, 2 * PAIRS, P], F32)
             first_word = (PACK * c + 2 * s) * PAIRS
             for slot in range(2 * PAIRS):
                 nc.tensor.transpose(xt[:, slot, :], x_words[:, first_word + slot, :], ident[:])
             xT_words = xT[u][:].rearrange("i (j b h) -> i j b h", j=PACK, h=PAIRS)
-            nc.vector.tensor_copy(
-                out=xT_words[:, 2 * s : 2 * s + 2, :, :],
-                in_=xt[:].rearrange("i (j h) b -> i j b h", h=PAIRS),
+            empty_bank(
+                s == 0,
+                xT_words[:, 2 * s : 2 * s + 2, :, :],
+                xt[:].rearrange("i (j h) b -> i j b h", h=PAIRS),
             )
 
         def first_contraction(u, q):
@@ -99,7 +106,8 @@ def tile_ttmatrix_s_kernel(tc, vector, core0, core1, core2, out):
             x_cols = xT[u][:].bitcast(BF16).rearrange("i (j w) -> i j w", j=PACK)
             h0 = h0_banks.tile([P, PACK, BANK_COLS], F32, tag="h0")
             nc.tensor.matmul(out=h0[:], lhsT=core0_p[:], rhs=x_cols[:, :, cols], start=True, stop=True)
-            nc.scalar.copy(out=h0_bf[u][:, cols, :], in_=h0[:].rearrange("p j w -> p w j"))
+            by_vector = q == 0 or (q == 2 and u + AHEAD >= UNITS)
+            empty_bank(by_vector, h0_bf[u][:, cols, :], h0[:].rearrange("p j w -> p w j"))
 
         def quantise_h0(u, half):
             cols = slice(half * HALF, (half + 1) * HALF)
@@ -109,10 +117,21 @@ def tile_ttmatrix_s_kernel(tc, vector, core0, core1, core2, out):
                 in_=h0_bf[u][:, cols, :].rearrange("p w j -> p (w j)"),
             )
 
-        def second_and_third_contraction(bt):
+        def work_unit(u):
+            first_contraction(u, 0)
+            first_contraction(u, 1)
+            quantise_h0(u, 0)
+            first_contraction(u, 2)
+            first_contraction(u, 3)
+            if u + AHEAD < UNITS:
+                transpose_words(u + AHEAD, 0)
+                transpose_words(u + AHEAD, 1)
+            quantise_h0(u, 1)
+
+        def second_contraction(bt):
             h1 = h1_banks.tile([R2, COLS], F32)
             for c in range(PASSES):
-                u = units.index((bt, c))
+                u = bt * PASSES + c
                 nc.tensor.matmul_mx(
                     out=h1[:],
                     lhsT=w1_codes[:, c, :].bitcast(FP8X4),
@@ -123,16 +142,17 @@ def tile_ttmatrix_s_kernel(tc, vector, core0, core1, core2, out):
                     stop=(c == PASSES - 1),
                 )
             h1_bf = keep.tile([R2, COLS], BF16, name="h1_bf%d" % bt, align_bytes=64)
-            h1_codes = keep.tile([R2, P], U32, name="h1_codes%d" % bt, align_bytes=64)
-            h1_scales = keep.tile([R2, P], U8, name="h1_scales%d" % bt, align_bytes=64)
             nc.scalar.copy(out=h1_bf[:], in_=h1[:])
-            nc.vector.quantize_mx(out=h1_codes[:].bitcast(FP8X4), scales=h1_scales[:], in_=h1_bf[:])
+            nc.vector.quantize_mx(
+                out=h1_codes[bt][:].bitcast(FP8X4), scales=h1_scales[bt][:], in_=h1_bf[:]
+            )
 
+        def third_contraction(bt):
             acc = out_banks.tile([P, O2], F32)
             nc.tensor.matmul_mx(
                 out=acc[:],
-                lhsT=h1_codes[:].bitcast(FP8X4),
-                lhsT_scale=h1_scales[:],
+                lhsT=h1_codes[bt][:].bitcast(FP8X4),
+                lhsT_scale=h1_scales[bt][:],
                 rhs=w2_codes[:].bitcast(FP8X4),
                 rhs_scale=w2_scales[:],
                 start=True,
@@ -144,9 +164,10 @@ def tile_ttmatrix_s_kernel(tc, vector, core0, core1, core2, out):
                 out=out.rearrange("b x y o -> b (x y o)")[bt * P : (bt + 1) * P, :], in_=out_sb[:]
             )
 
-        transpose_words(0, 0)
-        transpose_words(0, 1)
-
+        ident = keep.tile([P, P], F32)
+        make_identity(nc, ident[:])
+        rank_select = keep.tile([R1, P], BF16)
+        nc.vector.tensor_copy(out=partitions_split(rank_select[:]), in_=ranks_by_partition(ident[:]))
         core0_p = keep.tile([I0, P], BF16)
         nc.vector.tensor_copy(out=partitions_split(core0_p[:]), in_=ranks_by_partition(core0_sb[:]))
 
@@ -166,17 +187,17 @@ def tile_ttmatrix_s_kernel(tc, vector, core0, core1, core2, out):
             in_=w1_bf[:].rearrange("p c k j -> p (c k j)"),
         )
 
+        for u in range(AHEAD):
+            transpose_words(u, 0)
+            transpose_words(u, 1)
+        work_unit(0)
+        work_unit(1)
+        work_unit(2)
         w2_codes = keep.tile([R2, O2], U32, align_bytes=64)
         w2_scales = keep.tile([R2, O2], U8, align_bytes=64)
         nc.vector.quantize_mx(out=w2_codes[:].bitcast(FP8X4), scales=w2_scales[:], in_=core2_sb[:])
-
-        for u in range(len(units)):
-            for half in range(2):
-                for q in range(half * BANKS // 2, (half + 1) * BANKS // 2):
-                    first_contraction(u, q)
-                if u + 1 < len(units):
-                    transpose_words(u + 1, half)
-                quantise_h0(u, half)
-            bt, c = units[u]
-            if c == PASSES - 1:
-                second_and_third_contraction(bt)
+        second_contraction(0)
+        work_unit(3)
+        third_contraction(0)
+        second_contraction(1)
+        third_contraction(1)

@@ -11,7 +11,6 @@ FP8X4 = mybir.dt.float8_e4m3fn_x4
 
 P = 128
 PACK = 4
-BANK = 512
 
 B, I0, I1, I2 = 256, 128, 8, 4
 R1, R2, O2 = 128, 128, 128
@@ -21,10 +20,10 @@ PASSES = I1 // PACK
 PAIRS = I2 // 2
 WORDS = I1 * PAIRS
 COLS = P * I2
-BANK_COLS = BANK // PACK
-HALF = COLS // 2
-UNITS = B_TILES * PASSES
-AHEAD = 2
+
+SLABS = B_TILES * PASSES * PAIRS
+SLAB_COLS = COLS // PAIRS
+AHEAD = 3
 
 RUN = 4
 RUNS = 4
@@ -46,8 +45,8 @@ def tile_ttmatrix_s_kernel(tc, vector, core0, core1, core2, out):
 
     with ExitStack() as ctx:
         keep = ctx.enter_context(tc.tile_pool(name="keep", bufs=1))
-        xt_banks = ctx.enter_context(tc.psum_pool(name="xt_banks", bufs=2))
-        h0_banks = ctx.enter_context(tc.psum_pool(name="h0_banks", bufs=4))
+        xt_banks = ctx.enter_context(tc.psum_pool(name="xt_banks", bufs=3))
+        h0_banks = ctx.enter_context(tc.psum_pool(name="h0_banks", bufs=3))
         h1_banks = ctx.enter_context(tc.psum_pool(name="h1_banks", bufs=1))
         out_banks = ctx.enter_context(tc.psum_pool(name="out_banks", bufs=1))
 
@@ -64,15 +63,18 @@ def tile_ttmatrix_s_kernel(tc, vector, core0, core1, core2, out):
             nc.sync.dma_start(out=x_sb[bt][:], in_=x_rows[bt * P : (bt + 1) * P, :])
         nc.sync.dma_start(out=core2_sb[:], in_=core2.rearrange("r o i x -> r (o i x)"))
 
-        xT = [keep.tile([I0, PACK * P * PAIRS], F32, name="xT%d" % u) for u in range(UNITS)]
+        xT = [keep.tile([I0, P * PACK], F32, name="xT%d" % k) for k in range(SLABS)]
         h0_bf = [
-            keep.tile([P, COLS, PACK], BF16, name="h0_bf%d" % u, align_bytes=64) for u in range(UNITS)
+            keep.tile([P, SLAB_COLS * PACK], BF16, name="h0_bf%d" % k, align_bytes=64)
+            for k in range(SLABS)
         ]
         h0_codes = [
-            keep.tile([P, COLS], U32, name="h0_codes%d" % u, align_bytes=64) for u in range(UNITS)
+            keep.tile([P, COLS], U32, name="h0_codes%d" % u, align_bytes=64)
+            for u in range(B_TILES * PASSES)
         ]
         h0_scales = [
-            keep.tile([P, COLS], U8, name="h0_scales%d" % u, align_bytes=64) for u in range(UNITS)
+            keep.tile([P, COLS], U8, name="h0_scales%d" % u, align_bytes=64)
+            for u in range(B_TILES * PASSES)
         ]
         h1_codes = [
             keep.tile([R2, P], U32, name="h1_codes%d" % bt, align_bytes=64) for bt in range(B_TILES)
@@ -81,52 +83,44 @@ def tile_ttmatrix_s_kernel(tc, vector, core0, core1, core2, out):
             keep.tile([R2, P], U8, name="h1_scales%d" % bt, align_bytes=64) for bt in range(B_TILES)
         ]
 
-        def empty_bank(by_vector, out_ap, bank_ap):
-            if by_vector:
-                nc.vector.tensor_copy(out=out_ap, in_=bank_ap)
-            else:
-                nc.scalar.copy(out=out_ap, in_=bank_ap)
-
-        def transpose_words(u, s):
+        def transpose_words(k, xt, i1_range):
+            u, h = divmod(k, PAIRS)
             bt, c = divmod(u, PASSES)
             x_words = x_sb[bt][:].bitcast(F32).rearrange("b (i w) -> b w i", w=WORDS)
-            xt = xt_banks.tile([I0, 2 * PAIRS, P], F32)
-            first_word = (PACK * c + 2 * s) * PAIRS
-            for slot in range(2 * PAIRS):
-                nc.tensor.transpose(xt[:, slot, :], x_words[:, first_word + slot, :], ident[:])
-            xT_words = xT[u][:].rearrange("i (j b h) -> i j b h", j=PACK, h=PAIRS)
-            empty_bank(
-                s == 0,
-                xT_words[:, 2 * s : 2 * s + 2, :, :],
-                xt[:].rearrange("i (j h) b -> i j b h", h=PAIRS),
+            for j in i1_range:
+                nc.tensor.transpose(xt[:, j, :], x_words[:, (PACK * c + j) * PAIRS + h, :], ident[:])
+
+        def empty_transposes(k, xt):
+            nc.vector.tensor_copy(
+                out=xT[k][:].rearrange("i (b j) -> i b j", j=PACK), in_=xt[:].rearrange("i j b -> i b j")
             )
 
-        def first_contraction(u, q):
-            cols = slice(q * BANK_COLS, (q + 1) * BANK_COLS)
-            x_cols = xT[u][:].bitcast(BF16).rearrange("i (j w) -> i j w", j=PACK)
-            h0 = h0_banks.tile([P, PACK, BANK_COLS], F32, tag="h0")
-            nc.tensor.matmul(out=h0[:], lhsT=core0_p[:], rhs=x_cols[:, :, cols], start=True, stop=True)
-            by_vector = q == 0 or (q == 2 and u + AHEAD >= UNITS)
-            empty_bank(by_vector, h0_bf[u][:, cols, :], h0[:].rearrange("p j w -> p w j"))
-
-        def quantise_h0(u, half):
-            cols = slice(half * HALF, (half + 1) * HALF)
+        def work_slab(k):
+            u, h = divmod(k, PAIRS)
+            transposing = k + AHEAD < SLABS
+            if transposing:
+                xt = xt_banks.tile([I0, PACK, P], F32, tag="xt")
+            x_cols = xT[k][:].bitcast(BF16).rearrange("i (b j e) -> i b e j", j=PACK, e=2)
+            h0 = h0_banks.tile([P, SLAB_COLS * PACK], BF16)
+            h0_cols = h0[:].rearrange("p (b e j) -> p b e j", j=PACK, e=2)
+            for half in range(2):
+                b_range = slice(half * P // 2, (half + 1) * P // 2)
+                nc.tensor.matmul(
+                    out=h0_cols[:, b_range, :, :],
+                    lhsT=core0_p[:],
+                    rhs=x_cols[:, b_range, :, :],
+                    start=True,
+                    stop=True,
+                )
+                if transposing:
+                    transpose_words(k + AHEAD, xt, range(half * PACK // 2, (half + 1) * PACK // 2))
+            nc.scalar.copy(out=h0_bf[k][:], in_=h0[:])
+            if transposing:
+                empty_transposes(k + AHEAD, xt)
+            cols = slice(h * SLAB_COLS, (h + 1) * SLAB_COLS)
             nc.vector.quantize_mx(
-                out=h0_codes[u][:, cols].bitcast(FP8X4),
-                scales=h0_scales[u][:, cols],
-                in_=h0_bf[u][:, cols, :].rearrange("p w j -> p (w j)"),
+                out=h0_codes[u][:, cols].bitcast(FP8X4), scales=h0_scales[u][:, cols], in_=h0_bf[k][:]
             )
-
-        def work_unit(u):
-            first_contraction(u, 0)
-            first_contraction(u, 1)
-            quantise_h0(u, 0)
-            first_contraction(u, 2)
-            first_contraction(u, 3)
-            if u + AHEAD < UNITS:
-                transpose_words(u + AHEAD, 0)
-                transpose_words(u + AHEAD, 1)
-            quantise_h0(u, 1)
 
         def second_contraction(bt):
             h1 = h1_banks.tile([R2, COLS], F32)
@@ -142,7 +136,10 @@ def tile_ttmatrix_s_kernel(tc, vector, core0, core1, core2, out):
                     stop=(c == PASSES - 1),
                 )
             h1_bf = keep.tile([R2, COLS], BF16, name="h1_bf%d" % bt, align_bytes=64)
-            nc.scalar.copy(out=h1_bf[:], in_=h1[:])
+            nc.scalar.copy(
+                out=h1_bf[:].rearrange("r (b h e) -> r b h e", h=PAIRS, e=2),
+                in_=h1[:].rearrange("r (h b e) -> r b h e", h=PAIRS, e=2),
+            )
             nc.vector.quantize_mx(
                 out=h1_codes[bt][:].bitcast(FP8X4), scales=h1_scales[bt][:], in_=h1_bf[:]
             )
@@ -176,7 +173,7 @@ def tile_ttmatrix_s_kernel(tc, vector, core0, core1, core2, out):
         w1_scales = keep.tile([P, PASSES, R2], U8, align_bytes=64)
         core1_passes = core1_sb[:].rearrange("r (c j k) -> r c j k", c=PASSES, j=PACK)
         for c in range(PASSES):
-            w1_rows = h0_banks.tile([P, PACK, R2], F32, tag="h0")
+            w1_rows = xt_banks.tile([P, PACK, R2], F32, tag="xt")
             nc.tensor.matmul(
                 out=w1_rows[:], lhsT=rank_select[:], rhs=core1_passes[:, c, :, :], start=True, stop=True
             )
@@ -187,17 +184,17 @@ def tile_ttmatrix_s_kernel(tc, vector, core0, core1, core2, out):
             in_=w1_bf[:].rearrange("p c k j -> p (c k j)"),
         )
 
-        for u in range(AHEAD):
-            transpose_words(u, 0)
-            transpose_words(u, 1)
-        work_unit(0)
-        work_unit(1)
-        work_unit(2)
+        for k in range(AHEAD):
+            xt = xt_banks.tile([I0, PACK, P], F32, tag="xt")
+            transpose_words(k, xt, range(PACK))
+            empty_transposes(k, xt)
+        for k in range(SLABS - 1):
+            work_slab(k)
         w2_codes = keep.tile([R2, O2], U32, align_bytes=64)
         w2_scales = keep.tile([R2, O2], U8, align_bytes=64)
         nc.vector.quantize_mx(out=w2_codes[:].bitcast(FP8X4), scales=w2_scales[:], in_=core2_sb[:])
         second_contraction(0)
-        work_unit(3)
+        work_slab(SLABS - 1)
         third_contraction(0)
         second_contraction(1)
         third_contraction(1)

@@ -101,20 +101,16 @@ def tile_ttmatrix_s_kernel(tc, vector, core0, core1, core2, out):
             if transposing:
                 xt = xt_banks.tile([I0, PACK, P], F32, tag="xt")
             x_cols = xT[k][:].bitcast(BF16).rearrange("i (b j e) -> i b e j", j=PACK, e=2)
-            h0 = h0_banks.tile([P, SLAB_COLS * PACK], BF16)
-            h0_cols = h0[:].rearrange("p (b e j) -> p b e j", j=PACK, e=2)
+            h0_out = h0_bf[k][:].rearrange("p (b e j) -> p b e j", j=PACK, e=2)
             for half in range(2):
                 b_range = slice(half * P // 2, (half + 1) * P // 2)
+                h0 = h0_banks.tile([P, P // 2, 2, PACK], F32)
                 nc.tensor.matmul(
-                    out=h0_cols[:, b_range, :, :],
-                    lhsT=core0_p[:],
-                    rhs=x_cols[:, b_range, :, :],
-                    start=True,
-                    stop=True,
+                    out=h0[:], lhsT=core0_p[:], rhs=x_cols[:, b_range, :, :], start=True, stop=True
                 )
+                nc.scalar.copy(out=h0_out[:, b_range, :, :], in_=h0[:])
                 if transposing:
                     transpose_words(k + AHEAD, xt, range(half * PACK // 2, (half + 1) * PACK // 2))
-            nc.scalar.copy(out=h0_bf[k][:], in_=h0[:])
             if transposing:
                 empty_transposes(k + AHEAD, xt)
             cols = slice(h * SLAB_COLS, (h + 1) * SLAB_COLS)

@@ -91,9 +91,11 @@ def tile_ttmatrix_s_kernel(tc, vector, core0, core1, core2, out):
                 nc.tensor.transpose(xt[:, j, :], x_words[:, (PACK * c + j) * PAIRS + h, :], ident[:])
 
         def empty_transposes(k, xt):
-            nc.vector.tensor_copy(
-                out=xT[k][:].rearrange("i (b j) -> i b j", j=PACK), in_=xt[:].rearrange("i j b -> i b j")
-            )
+            xT_out = xT[k][:].rearrange("i (b j) -> i b j", j=PACK)
+            if k % (PASSES * PAIRS) == 1:
+                nc.scalar.copy(out=xT_out, in_=xt[:].rearrange("i j b -> i b j"))
+            else:
+                nc.vector.tensor_copy(out=xT_out, in_=xt[:].rearrange("i j b -> i b j"))
 
         def work_slab(k):
             u, h = divmod(k, PAIRS)
@@ -101,16 +103,20 @@ def tile_ttmatrix_s_kernel(tc, vector, core0, core1, core2, out):
             if transposing:
                 xt = xt_banks.tile([I0, PACK, P], F32, tag="xt")
             x_cols = xT[k][:].bitcast(BF16).rearrange("i (b j e) -> i b e j", j=PACK, e=2)
-            h0_out = h0_bf[k][:].rearrange("p (b e j) -> p b e j", j=PACK, e=2)
+            h0 = h0_banks.tile([P, SLAB_COLS * PACK], BF16)
+            h0_cols = h0[:].rearrange("p (b e j) -> p b e j", j=PACK, e=2)
             for half in range(2):
                 b_range = slice(half * P // 2, (half + 1) * P // 2)
-                h0 = h0_banks.tile([P, P // 2, 2, PACK], F32)
                 nc.tensor.matmul(
-                    out=h0[:], lhsT=core0_p[:], rhs=x_cols[:, b_range, :, :], start=True, stop=True
+                    out=h0_cols[:, b_range, :, :],
+                    lhsT=core0_p[:],
+                    rhs=x_cols[:, b_range, :, :],
+                    start=True,
+                    stop=True,
                 )
-                nc.scalar.copy(out=h0_out[:, b_range, :, :], in_=h0[:])
                 if transposing:
                     transpose_words(k + AHEAD, xt, range(half * PACK // 2, (half + 1) * PACK // 2))
+            nc.scalar.copy(out=h0_bf[k][:], in_=h0[:])
             if transposing:
                 empty_transposes(k + AHEAD, xt)
             cols = slice(h * SLAB_COLS, (h + 1) * SLAB_COLS)

@@ -58,9 +58,9 @@ def tile_ttmatrix_s_kernel(tc, vector, core0, core1, core2, out):
         core1_sb = keep.tile([R1, I1 * R2], BF16)
         core2_sb = keep.tile([R2, O2 * I2], BF16, align_bytes=64)
         nc.sync.dma_start(out=core0_sb[:], in_=core0.rearrange("a o i r -> (a o i) r"))
-        nc.sync.dma_start(out=core1_sb[:], in_=core1.rearrange("r o i k -> r (o i k)"))
         for bt in range(B_TILES):
             nc.sync.dma_start(out=x_sb[bt][:], in_=x_rows[bt * P : (bt + 1) * P, :])
+        nc.sync.dma_start(out=core1_sb[:], in_=core1.rearrange("r o i k -> r (o i k)"))
         nc.sync.dma_start(out=core2_sb[:], in_=core2.rearrange("r o i x -> r (o i x)"))
 
         xT = [keep.tile([I0, P * PACK], F32, name="xT%d" % k) for k in range(SLABS)]
@@ -103,7 +103,7 @@ def tile_ttmatrix_s_kernel(tc, vector, core0, core1, core2, out):
             if transposing:
                 xt = xt_banks.tile([I0, PACK, P], F32, tag="xt")
             x_cols = xT[k][:].bitcast(BF16).rearrange("i (b j e) -> i b e j", j=PACK, e=2)
-            h0 = h0_banks.tile([P, SLAB_COLS * PACK], BF16)
+            h0 = h0_banks.tile([P, SLAB_COLS * PACK], BF16, tag="h0")
             h0_cols = h0[:].rearrange("p (b e j) -> p b e j", j=PACK, e=2)
             for half in range(2):
                 b_range = slice(half * P // 2, (half + 1) * P // 2)
@@ -122,6 +122,25 @@ def tile_ttmatrix_s_kernel(tc, vector, core0, core1, core2, out):
             cols = slice(h * SLAB_COLS, (h + 1) * SLAB_COLS)
             nc.vector.quantize_mx(
                 out=h0_codes[u][:, cols].bitcast(FP8X4), scales=h0_scales[u][:, cols], in_=h0_bf[k][:]
+            )
+
+        w1_codes = keep.tile([P, PASSES, R2], U32, align_bytes=64)
+        w1_scales = keep.tile([P, PASSES, R2], U8, align_bytes=64)
+
+        def prepare_core1():
+            w1_rows = h0_banks.tile([P, PASSES, R2, PACK], BF16, tag="h0")
+            core1_passes = core1_sb[:].rearrange("r (c j k) -> r c k j", c=PASSES, j=PACK)
+            for c in range(PASSES):
+                nc.tensor.matmul(
+                    out=w1_rows[:, c, :, :], lhsT=rank_select[:], rhs=core1_passes[:, c, :, :],
+                    start=True, stop=True,
+                )
+            w1_bf = keep.tile([P, PASSES * R2 * PACK], BF16, align_bytes=64)
+            nc.scalar.copy(out=w1_bf[:], in_=w1_rows[:].rearrange("p c k j -> p (c k j)"))
+            nc.vector.quantize_mx(
+                out=w1_codes[:].rearrange("p c k -> p (c k)").bitcast(FP8X4),
+                scales=w1_scales[:].rearrange("p c k -> p (c k)"),
+                in_=w1_bf[:],
             )
 
         def second_contraction(bt):
@@ -170,28 +189,14 @@ def tile_ttmatrix_s_kernel(tc, vector, core0, core1, core2, out):
         core0_p = keep.tile([I0, P], BF16)
         nc.vector.tensor_copy(out=partitions_split(core0_p[:]), in_=ranks_by_partition(core0_sb[:]))
 
-        w1_bf = keep.tile([P, PASSES, R2, PACK], BF16, align_bytes=64)
-        w1_codes = keep.tile([P, PASSES, R2], U32, align_bytes=64)
-        w1_scales = keep.tile([P, PASSES, R2], U8, align_bytes=64)
-        core1_passes = core1_sb[:].rearrange("r (c j k) -> r c j k", c=PASSES, j=PACK)
-        for c in range(PASSES):
-            w1_rows = xt_banks.tile([P, PACK, R2], F32, tag="xt")
-            nc.tensor.matmul(
-                out=w1_rows[:], lhsT=rank_select[:], rhs=core1_passes[:, c, :, :], start=True, stop=True
-            )
-            nc.scalar.copy(out=w1_bf[:, c, :, :], in_=w1_rows[:].rearrange("p j k -> p k j"))
-        nc.vector.quantize_mx(
-            out=w1_codes[:].rearrange("p c k -> p (c k)").bitcast(FP8X4),
-            scales=w1_scales[:].rearrange("p c k -> p (c k)"),
-            in_=w1_bf[:].rearrange("p c k j -> p (c k j)"),
-        )
-
         for k in range(AHEAD):
             xt = xt_banks.tile([I0, PACK, P], F32, tag="xt")
             transpose_words(k, xt, range(PACK))
             empty_transposes(k, xt)
         for k in range(SLABS - 1):
             work_slab(k)
+            if k == PASSES * PAIRS:
+                prepare_core1()
         w2_codes = keep.tile([R2, O2], U32, align_bytes=64)
         w2_scales = keep.tile([R2, O2], U8, align_bytes=64)
         nc.vector.quantize_mx(out=w2_codes[:].bitcast(FP8X4), scales=w2_scales[:], in_=core2_sb[:])

@@ -5,6 +5,7 @@ from concourse.masks import make_identity
 
 F32 = mybir.dt.float32
 BF16 = mybir.dt.bfloat16
+ALU = mybir.AluOpType
 U32 = mybir.dt.uint32
 U8 = mybir.dt.uint8
 FP8X4 = mybir.dt.float8_e4m3fn_x4
@@ -23,6 +24,7 @@ COLS = P * I2
 
 SLABS = B_TILES * PASSES * PAIRS
 SLAB_COLS = COLS // PAIRS
+WARM_MATMULS = 8
 AHEAD = 3
 
 RUN = 4
@@ -55,12 +57,14 @@ def tile_ttmatrix_s_kernel(tc, vector, core0, core1, core2, out):
         x_rows = vector.rearrange("b i j k -> b (i j k)")
         x_sb = [keep.tile([P, I0 * I1 * I2], BF16, name="x_sb%d" % bt) for bt in range(B_TILES)]
         core0_sb = keep.tile([I0, R1], BF16)
-        core1_sb = keep.tile([R1, I1 * R2], BF16)
+        core1_sb = keep.tile([P, I1 * R2], BF16)
         core2_sb = keep.tile([R2, O2 * I2], BF16, align_bytes=64)
         nc.sync.dma_start(out=core0_sb[:], in_=core0.rearrange("a o i r -> (a o i) r"))
         for bt in range(B_TILES):
             nc.sync.dma_start(out=x_sb[bt][:], in_=x_rows[bt * P : (bt + 1) * P, :])
-        nc.sync.dma_start(out=core1_sb[:], in_=core1.rearrange("r o i k -> r (o i k)"))
+        core1_runs = core1.rearrange("(g n v) o i k -> n g v (o i k)", g=GROUPS, n=RUNS, v=RUN)
+        for n in range(RUNS):
+            nc.sync.dma_start(out=core1_sb[n * P // RUNS : (n + 1) * P // RUNS, :], in_=core1_runs[n])
         nc.sync.dma_start(out=core2_sb[:], in_=core2.rearrange("r o i x -> r (o i x)"))
 
         xT = [keep.tile([I0, P * PACK], F32, name="xT%d" % k) for k in range(SLABS)]
@@ -127,20 +131,27 @@ def tile_ttmatrix_s_kernel(tc, vector, core0, core1, core2, out):
         w1_codes = keep.tile([P, PASSES, R2], U32, align_bytes=64)
         w1_scales = keep.tile([P, PASSES, R2], U8, align_bytes=64)
 
-        def prepare_core1():
-            w1_rows = h0_banks.tile([P, PASSES, R2, PACK], BF16, tag="h0")
-            core1_passes = core1_sb[:].rearrange("r (c j k) -> r c k j", c=PASSES, j=PACK)
+        w1_bf = keep.tile([P, PASSES, R2, PACK], BF16, align_bytes=64)
+
+        def interleave_core1():
+            core1_passes = core1_sb[:].rearrange("p (c j k) -> p c k j", c=PASSES, j=PACK)
             for c in range(PASSES):
-                nc.tensor.matmul(
-                    out=w1_rows[:, c, :, :], lhsT=rank_select[:], rhs=core1_passes[:, c, :, :],
-                    start=True, stop=True,
-                )
-            w1_bf = keep.tile([P, PASSES * R2 * PACK], BF16, align_bytes=64)
-            nc.scalar.copy(out=w1_bf[:], in_=w1_rows[:].rearrange("p c k j -> p (c k j)"))
+                for k_half in range(2):
+                    k_range = slice(k_half * R2 // 2, (k_half + 1) * R2 // 2)
+                    nc.gpsimd.tensor_scalar(
+                        out=w1_bf[:, c, k_range, :],
+                        in0=core1_passes[:, c, k_range, :],
+                        scalar1=1.0,
+                        scalar2=0.0,
+                        op0=ALU.mult,
+                        op1=ALU.add,
+                    )
+
+        def quantise_core1():
             nc.vector.quantize_mx(
                 out=w1_codes[:].rearrange("p c k -> p (c k)").bitcast(FP8X4),
                 scales=w1_scales[:].rearrange("p c k -> p (c k)"),
-                in_=w1_bf[:],
+                in_=w1_bf[:].rearrange("p c k j -> p (c k j)"),
             )
 
         def second_contraction(bt):
@@ -166,7 +177,7 @@ def tile_ttmatrix_s_kernel(tc, vector, core0, core1, core2, out):
             )
 
         def third_contraction(bt):
-            acc = out_banks.tile([P, O2], F32)
+            acc = out_banks.tile([P, O2], F32, tag="acc")
             nc.tensor.matmul_mx(
                 out=acc[:],
                 lhsT=h1_codes[bt][:].bitcast(FP8X4),
@@ -184,10 +195,13 @@ def tile_ttmatrix_s_kernel(tc, vector, core0, core1, core2, out):
 
         ident = keep.tile([P, P], F32)
         make_identity(nc, ident[:])
-        rank_select = keep.tile([R1, P], BF16)
-        nc.vector.tensor_copy(out=partitions_split(rank_select[:]), in_=ranks_by_partition(ident[:]))
         core0_p = keep.tile([I0, P], BF16)
         nc.vector.tensor_copy(out=partitions_split(core0_p[:]), in_=ranks_by_partition(core0_sb[:]))
+
+        interleave_core1()
+        warm = out_banks.tile([P, P], F32, tag="acc")
+        for i in range(WARM_MATMULS):
+            nc.tensor.matmul(out=warm[:], lhsT=ident[:], rhs=ident[:], start=True, stop=True)
 
         for k in range(AHEAD):
             xt = xt_banks.tile([I0, PACK, P], F32, tag="xt")
@@ -196,7 +210,7 @@ def tile_ttmatrix_s_kernel(tc, vector, core0, core1, core2, out):
         for k in range(SLABS - 1):
             work_slab(k)
             if k == PASSES * PAIRS:
-                prepare_core1()
+                quantise_core1()
         w2_codes = keep.tile([R2, O2], U32, align_bytes=64)
         w2_scales = keep.tile([R2, O2], U8, align_bytes=64)
         nc.vector.quantize_mx(out=w2_codes[:].bitcast(FP8X4), scales=w2_scales[:], in_=core2_sb[:])

@@ -5,7 +5,6 @@ from concourse.masks import make_identity
 
 F32 = mybir.dt.float32
 BF16 = mybir.dt.bfloat16
-ALU = mybir.AluOpType
 U32 = mybir.dt.uint32
 U8 = mybir.dt.uint8
 FP8X4 = mybir.dt.float8_e4m3fn_x4
@@ -24,8 +23,8 @@ COLS = P * I2
 
 SLABS = B_TILES * PASSES * PAIRS
 SLAB_COLS = COLS // PAIRS
-WARM_MATMULS = 8
-AHEAD = 3
+WARM_MATMULS = 6
+AHEAD = 2
 
 RUN = 4
 RUNS = 4
@@ -133,19 +132,9 @@ def tile_ttmatrix_s_kernel(tc, vector, core0, core1, core2, out):
 
         w1_bf = keep.tile([P, PASSES, R2, PACK], BF16, align_bytes=64)
 
-        def interleave_core1():
+        def interleave_core1(c):
             core1_passes = core1_sb[:].rearrange("p (c j k) -> p c k j", c=PASSES, j=PACK)
-            for c in range(PASSES):
-                for k_half in range(2):
-                    k_range = slice(k_half * R2 // 2, (k_half + 1) * R2 // 2)
-                    nc.gpsimd.tensor_scalar(
-                        out=w1_bf[:, c, k_range, :],
-                        in0=core1_passes[:, c, k_range, :],
-                        scalar1=1.0,
-                        scalar2=0.0,
-                        op0=ALU.mult,
-                        op1=ALU.add,
-                    )
+            nc.vector.tensor_copy(out=w1_bf[:, c, :, :], in_=core1_passes[:, c, :, :])
 
         def quantise_core1():
             nc.vector.quantize_mx(
@@ -198,18 +187,24 @@ def tile_ttmatrix_s_kernel(tc, vector, core0, core1, core2, out):
         core0_p = keep.tile([I0, P], BF16)
         nc.vector.tensor_copy(out=partitions_split(core0_p[:]), in_=ranks_by_partition(core0_sb[:]))
 
-        interleave_core1()
         warm = out_banks.tile([P, P], F32, tag="acc")
-        for i in range(WARM_MATMULS):
-            nc.tensor.matmul(out=warm[:], lhsT=ident[:], rhs=ident[:], start=True, stop=True)
+
+        def keep_warm(count):
+            for i in range(count):
+                nc.tensor.matmul(out=warm[:], lhsT=ident[:], rhs=ident[:], start=True, stop=True)
+
+        keep_warm(WARM_MATMULS)
 
         for k in range(AHEAD):
             xt = xt_banks.tile([I0, PACK, P], F32, tag="xt")
             transpose_words(k, xt, range(PACK))
+            keep_warm(1)
             empty_transposes(k, xt)
         for k in range(SLABS - 1):
             work_slab(k)
-            if k == PASSES * PAIRS:
+            if k == AHEAD or k == AHEAD + 1:
+                interleave_core1(k - AHEAD)
+            elif k == AHEAD + PASSES:
                 quantise_core1()
         w2_codes = keep.tile([R2, O2], U32, align_bytes=64)
         w2_scales = keep.tile([R2, O2], U8, align_bytes=64)

@@ -21,10 +21,12 @@ PAIRS = I2 // 2
 WORDS = I1 * PAIRS
 COLS = P * I2
 
-SLABS = B_TILES * PASSES * PAIRS
-SLAB_COLS = COLS // PAIRS
-WARM_MATMULS = 6
-AHEAD = 2
+GROUPS_T = B_TILES * PASSES * PAIRS
+HALVES = 2
+HALF = P // HALVES
+SLABS = B_TILES * PASSES * HALVES
+SLAB_COLS = HALF * I2
+AHEAD = 3
 
 RUN = 4
 RUNS = 4
@@ -66,10 +68,10 @@ def tile_ttmatrix_s_kernel(tc, vector, core0, core1, core2, out):
             nc.sync.dma_start(out=core1_sb[n * P // RUNS : (n + 1) * P // RUNS, :], in_=core1_runs[n])
         nc.sync.dma_start(out=core2_sb[:], in_=core2.rearrange("r o i x -> r (o i x)"))
 
-        xT = [keep.tile([I0, P * PACK], F32, name="xT%d" % k) for k in range(SLABS)]
+        xT = [keep.tile([I0, P * PACK], F32, name="xT%d" % k) for k in range(GROUPS_T)]
         h0_bf = [
-            keep.tile([P, SLAB_COLS * PACK], BF16, name="h0_bf%d" % k, align_bytes=64)
-            for k in range(SLABS)
+            keep.tile([P, SLAB_COLS * PACK], BF16, name="h0_bf%d" % s, align_bytes=64)
+            for s in range(SLABS)
         ]
         h0_codes = [
             keep.tile([P, COLS], U32, name="h0_codes%d" % u, align_bytes=64)
@@ -95,36 +97,51 @@ def tile_ttmatrix_s_kernel(tc, vector, core0, core1, core2, out):
 
         def empty_transposes(k, xt):
             xT_out = xT[k][:].rearrange("i (b j) -> i b j", j=PACK)
-            if k % (PASSES * PAIRS) == 1:
+            if k in (1, 4, 6):
                 nc.scalar.copy(out=xT_out, in_=xt[:].rearrange("i j b -> i b j"))
             else:
                 nc.vector.tensor_copy(out=xT_out, in_=xt[:].rearrange("i j b -> i b j"))
 
-        def work_slab(k):
-            u, h = divmod(k, PAIRS)
-            transposing = k + AHEAD < SLABS
+        def multiply_slab(s):
+            u, bh = divmod(s, HALVES)
+            transposing = s + AHEAD < GROUPS_T
+            last = s == SLABS - 1
             if transposing:
                 xt = xt_banks.tile([I0, PACK, P], F32, tag="xt")
-            x_cols = xT[k][:].bitcast(BF16).rearrange("i (b j e) -> i b e j", j=PACK, e=2)
-            h0 = h0_banks.tile([P, SLAB_COLS * PACK], BF16, tag="h0")
-            h0_cols = h0[:].rearrange("p (b e j) -> p b e j", j=PACK, e=2)
-            for half in range(2):
-                b_range = slice(half * P // 2, (half + 1) * P // 2)
+            h0_out = h0_bf[s][:].rearrange("p (b h n) -> p h b n", b=HALF, h=PAIRS)
+            if not last:
+                h0 = h0_banks.tile([P, HALF, PAIRS, 2, PACK], BF16, tag="h0")
+            for h in range(PAIRS):
+                x_cols = xT[u * PAIRS + h][:].bitcast(BF16).rearrange(
+                    "i (b j e) -> i b e j", j=PACK, e=2
+                )
+                if last:
+                    h0_pair = h0_banks.tile([P, HALF, 2, PACK], BF16, tag="h0")
                 nc.tensor.matmul(
-                    out=h0_cols[:, b_range, :, :],
+                    out=h0_pair[:] if last else h0[:, :, h, :, :],
                     lhsT=core0_p[:],
-                    rhs=x_cols[:, b_range, :, :],
+                    rhs=x_cols[:, bh * HALF : (bh + 1) * HALF, :, :],
                     start=True,
                     stop=True,
                 )
                 if transposing:
-                    transpose_words(k + AHEAD, xt, range(half * PACK // 2, (half + 1) * PACK // 2))
-            nc.scalar.copy(out=h0_bf[k][:], in_=h0[:])
+                    transpose_words(s + AHEAD, xt, range(h * PACK // 2, (h + 1) * PACK // 2))
+                if last:
+                    h0_in = h0_pair[:].rearrange("p b e j -> p b (e j)")
+                    if h == 0:
+                        nc.scalar.copy(out=h0_out[:, h, :, :], in_=h0_in)
+                    else:
+                        nc.vector.tensor_copy(out=h0_out[:, h, :, :], in_=h0_in)
+            if not last:
+                nc.scalar.copy(out=h0_bf[s][:], in_=h0[:].rearrange("p b h e j -> p (b h e j)"))
             if transposing:
-                empty_transposes(k + AHEAD, xt)
-            cols = slice(h * SLAB_COLS, (h + 1) * SLAB_COLS)
+                empty_transposes(s + AHEAD, xt)
+
+        def quantise_slab(s):
+            u, bh = divmod(s, HALVES)
+            cols = slice(bh * SLAB_COLS, (bh + 1) * SLAB_COLS)
             nc.vector.quantize_mx(
-                out=h0_codes[u][:, cols].bitcast(FP8X4), scales=h0_scales[u][:, cols], in_=h0_bf[k][:]
+                out=h0_codes[u][:, cols].bitcast(FP8X4), scales=h0_scales[u][:, cols], in_=h0_bf[s][:]
             )
 
         w1_codes = keep.tile([P, PASSES, R2], U32, align_bytes=64)
@@ -143,30 +160,32 @@ def tile_ttmatrix_s_kernel(tc, vector, core0, core1, core2, out):
                 in_=w1_bf[:].rearrange("p c k j -> p (c k j)"),
             )
 
-        def second_contraction(bt):
-            h1 = h1_banks.tile([R2, COLS], F32)
-            for c in range(PASSES):
-                u = bt * PASSES + c
-                nc.tensor.matmul_mx(
-                    out=h1[:],
-                    lhsT=w1_codes[:, c, :].bitcast(FP8X4),
-                    lhsT_scale=w1_scales[:, c, :],
-                    rhs=h0_codes[u][:].bitcast(FP8X4),
-                    rhs_scale=h0_scales[u][:],
-                    start=(c == 0),
-                    stop=(c == PASSES - 1),
-                )
-            h1_bf = keep.tile([R2, COLS], BF16, name="h1_bf%d" % bt, align_bytes=64)
-            nc.scalar.copy(
-                out=h1_bf[:].rearrange("r (b h e) -> r b h e", h=PAIRS, e=2),
-                in_=h1[:].rearrange("r (h b e) -> r b h e", h=PAIRS, e=2),
-            )
-            nc.vector.quantize_mx(
-                out=h1_codes[bt][:].bitcast(FP8X4), scales=h1_scales[bt][:], in_=h1_bf[:]
+        h1_bf = [
+            keep.tile([R2, COLS], BF16, name="h1_bf%d" % bt, align_bytes=64) for bt in range(B_TILES)
+        ]
+
+        def multiply_core1(h1, bt, bh, c):
+            u = bt * PASSES + c
+            cols = slice(bh * SLAB_COLS, (bh + 1) * SLAB_COLS)
+            nc.tensor.matmul_mx(
+                out=h1,
+                lhsT=w1_codes[:, c, :].bitcast(FP8X4),
+                lhsT_scale=w1_scales[:, c, :],
+                rhs=h0_codes[u][:, cols].bitcast(FP8X4),
+                rhs_scale=h0_scales[u][:, cols],
+                start=(c == 0),
+                stop=(c == PASSES - 1),
             )
 
-        def third_contraction(bt):
-            acc = out_banks.tile([P, O2], F32, tag="acc")
+        def quantise_h1(bt, vectors):
+            cols = slice(vectors.start * I2, vectors.stop * I2)
+            nc.vector.quantize_mx(
+                out=h1_codes[bt][:, vectors].bitcast(FP8X4),
+                scales=h1_scales[bt][:, vectors],
+                in_=h1_bf[bt][:, cols],
+            )
+
+        def third_contraction(bt, acc):
             nc.tensor.matmul_mx(
                 out=acc[:],
                 lhsT=h1_codes[bt][:].bitcast(FP8X4),
@@ -176,10 +195,12 @@ def tile_ttmatrix_s_kernel(tc, vector, core0, core1, core2, out):
                 start=True,
                 stop=True,
             )
-            out_sb = keep.tile([P, O2], F32, name="out_sb%d" % bt)
-            nc.vector.tensor_copy(out=out_sb[:], in_=acc[:])
+
+        out_sb = [keep.tile([P, O2], F32, name="out_sb%d" % bt) for bt in range(B_TILES)]
+
+        def store(bt):
             nc.sync.dma_start(
-                out=out.rearrange("b x y o -> b (x y o)")[bt * P : (bt + 1) * P, :], in_=out_sb[:]
+                out=out.rearrange("b x y o -> b (x y o)")[bt * P : (bt + 1) * P, :], in_=out_sb[bt][:]
             )
 
         ident = keep.tile([P, P], F32)
@@ -187,30 +208,46 @@ def tile_ttmatrix_s_kernel(tc, vector, core0, core1, core2, out):
         core0_p = keep.tile([I0, P], BF16)
         nc.vector.tensor_copy(out=partitions_split(core0_p[:]), in_=ranks_by_partition(core0_sb[:]))
 
-        warm = out_banks.tile([P, P], F32, tag="acc")
-
-        def keep_warm(count):
-            for i in range(count):
-                nc.tensor.matmul(out=warm[:], lhsT=ident[:], rhs=ident[:], start=True, stop=True)
-
-        keep_warm(WARM_MATMULS)
+        w2_codes = keep.tile([R2, O2], U32, align_bytes=64)
+        w2_scales = keep.tile([R2, O2], U8, align_bytes=64)
 
         for k in range(AHEAD):
             xt = xt_banks.tile([I0, PACK, P], F32, tag="xt")
             transpose_words(k, xt, range(PACK))
-            keep_warm(1)
             empty_transposes(k, xt)
-        for k in range(SLABS - 1):
-            work_slab(k)
-            if k == AHEAD or k == AHEAD + 1:
-                interleave_core1(k - AHEAD)
-            elif k == AHEAD + PASSES:
+        for s in range(SLABS):
+            multiply_slab(s)
+            if s == SLABS - 1:
+                quantise_slab(s - 1)
+            if s != SLABS - 2:
+                quantise_slab(s)
+            if s in (2, 3):
+                interleave_core1(s - 2)
+            elif s == 4:
                 quantise_core1()
-        w2_codes = keep.tile([R2, O2], U32, align_bytes=64)
-        w2_scales = keep.tile([R2, O2], U8, align_bytes=64)
-        nc.vector.quantize_mx(out=w2_codes[:].bitcast(FP8X4), scales=w2_scales[:], in_=core2_sb[:])
-        second_contraction(0)
-        work_slab(SLABS - 1)
-        third_contraction(0)
-        second_contraction(1)
-        third_contraction(1)
+                nc.vector.quantize_mx(
+                    out=w2_codes[:].bitcast(FP8X4), scales=w2_scales[:], in_=core2_sb[:]
+                )
+
+        h1_first = h1_banks.tile([R2, COLS], F32, tag="h1")
+        for bh in range(HALVES):
+            for c in range(PASSES):
+                multiply_core1(h1_first[:, bh * SLAB_COLS : (bh + 1) * SLAB_COLS], 0, bh, c)
+        h1_last = [xt_banks.tile([R2, SLAB_COLS], F32, tag="xt", name="h1_last%d" % bh) for bh in range(HALVES)]
+        for c in range(PASSES):
+            for bh in range(HALVES):
+                multiply_core1(h1_last[bh][:], 1, bh, c)
+        nc.scalar.copy(out=h1_bf[0][:], in_=h1_first[:])
+        nc.vector.tensor_copy(out=h1_bf[1][:, 0:SLAB_COLS], in_=h1_last[0][:])
+        quantise_h1(0, slice(0, P))
+        nc.scalar.copy(out=h1_bf[1][:, SLAB_COLS:COLS], in_=h1_last[1][:])
+        for bh in range(HALVES):
+            quantise_h1(1, slice(bh * HALF, (bh + 1) * HALF))
+        acc_first = out_banks.tile([P, O2], F32, tag="acc")
+        third_contraction(0, acc_first)
+        acc_last = xt_banks.tile([P, O2], F32, tag="xt")
+        third_contraction(1, acc_last)
+        nc.scalar.copy(out=out_sb[0][:], in_=acc_first[:])
+        store(0)
+        nc.vector.tensor_copy(out=out_sb[1][:], in_=acc_last[:])
+        store(1)

@@ -88,11 +88,11 @@ def tile_ttmatrix_s_kernel(tc, vector, core0, core1, core2, out):
             keep.tile([R2, P], U8, name="h1_scales%d" % bt, align_bytes=64) for bt in range(B_TILES)
         ]
 
-        def transpose_words(k, xt, i1_range):
+        def transpose_words(k, xt):
             u, h = divmod(k, PAIRS)
             bt, c = divmod(u, PASSES)
             x_words = x_sb[bt][:].bitcast(F32).rearrange("b (i w) -> b w i", w=WORDS)
-            for j in i1_range:
+            for j in range(PACK):
                 nc.tensor.transpose(xt[:, j, :], x_words[:, (PACK * c + j) * PAIRS + h, :], ident[:])
 
         def empty_transposes(k, xt):
@@ -124,14 +124,14 @@ def tile_ttmatrix_s_kernel(tc, vector, core0, core1, core2, out):
                     start=True,
                     stop=True,
                 )
-                if transposing:
-                    transpose_words(s + AHEAD, xt, range(h * PACK // 2, (h + 1) * PACK // 2))
                 if last:
                     h0_in = h0_pair[:].rearrange("p b e j -> p b (e j)")
                     if h == 0:
                         nc.scalar.copy(out=h0_out[:, h, :, :], in_=h0_in)
                     else:
                         nc.vector.tensor_copy(out=h0_out[:, h, :, :], in_=h0_in)
+            if transposing:
+                transpose_words(s + AHEAD, xt)
             if not last:
                 nc.scalar.copy(out=h0_bf[s][:], in_=h0[:].rearrange("p b h e j -> p (b h e j)"))
             if transposing:
@@ -213,7 +213,7 @@ def tile_ttmatrix_s_kernel(tc, vector, core0, core1, core2, out):
 
         for k in range(AHEAD):
             xt = xt_banks.tile([I0, PACK, P], F32, tag="xt")
-            transpose_words(k, xt, range(PACK))
+            transpose_words(k, xt)
             empty_transposes(k, xt)
         for s in range(SLABS):
             multiply_slab(s)

from contextlib import ExitStack

import concourse.mybir as mybir
from concourse.masks import make_identity

F32 = mybir.dt.float32
BF16 = mybir.dt.bfloat16
U32 = mybir.dt.uint32
U8 = mybir.dt.uint8
FP8X4 = mybir.dt.float8_e4m3fn_x4

P = 128
PACK = 4

B, I0, I1, I2 = 256, 128, 8, 4
R1, R2, O2 = 128, 128, 128

B_TILES = B // P
PASSES = I1 // PACK
PAIRS = I2 // 2
WORDS = I1 * PAIRS
COLS = P * I2

GROUPS_T = B_TILES * PASSES * PAIRS
HALVES = 2
HALF = P // HALVES
SLABS = B_TILES * PASSES * HALVES
SLAB_COLS = HALF * I2
AHEAD = 3

RUN = 4
RUNS = 4
GROUPS = 8

FLOPS = 2 * B * I1 * I2 * I0 * R1 + 2 * B * I2 * R1 * I1 * R2 + 2 * B * R2 * I2 * O2


def ranks_by_partition(ap):
    return ap.rearrange("k (g n v) -> k n g v", g=GROUPS, n=RUNS, v=RUN)


def partitions_split(ap):
    return ap.rearrange("k (n g v) -> k n g v", g=GROUPS, n=RUNS, v=RUN)


def tile_ttmatrix_s_kernel(tc, vector, core0, core1, core2, out):
    nc = tc.nc

    with ExitStack() as ctx:
        keep = ctx.enter_context(tc.tile_pool(name="keep", bufs=1))
        xt_banks = ctx.enter_context(tc.psum_pool(name="xt_banks", bufs=3))
        h0_banks = ctx.enter_context(tc.psum_pool(name="h0_banks", bufs=3))
        h1_banks = ctx.enter_context(tc.psum_pool(name="h1_banks", bufs=1))
        out_banks = ctx.enter_context(tc.psum_pool(name="out_banks", bufs=1))

        ctx.enter_context(tc.manual_schedule())

        x_rows = vector.rearrange("b i j k -> b (i j k)")
        x_sb = [keep.tile([P, I0 * I1 * I2], BF16, name="x_sb%d" % bt) for bt in range(B_TILES)]
        core0_sb = keep.tile([I0, R1], BF16)
        core1_sb = keep.tile([P, I1 * R2], BF16)
        core2_sb = keep.tile([R2, O2 * I2], BF16, align_bytes=64)
        nc.sync.dma_start(out=core0_sb[:], in_=core0.rearrange("a o i r -> (a o i) r"))
        for bt in range(B_TILES):
            nc.sync.dma_start(out=x_sb[bt][:], in_=x_rows[bt * P : (bt + 1) * P, :])
        core1_runs = core1.rearrange("(g n v) o i k -> n g v (o i k)", g=GROUPS, n=RUNS, v=RUN)
        for n in range(RUNS):
            nc.sync.dma_start(out=core1_sb[n * P // RUNS : (n + 1) * P // RUNS, :], in_=core1_runs[n])
        nc.sync.dma_start(out=core2_sb[:], in_=core2.rearrange("r o i x -> r (o i x)"))

        xT = [keep.tile([I0, P * PACK], F32, name="xT%d" % k) for k in range(GROUPS_T)]
        h0_bf = [
            keep.tile([P, SLAB_COLS * PACK], BF16, name="h0_bf%d" % s, align_bytes=64)
            for s in range(SLABS)
        ]
        h0_codes = [
            keep.tile([P, COLS], U32, name="h0_codes%d" % u, align_bytes=64)
            for u in range(B_TILES * PASSES)
        ]
        h0_scales = [
            keep.tile([P, COLS], U8, name="h0_scales%d" % u, align_bytes=64)
            for u in range(B_TILES * PASSES)
        ]
        h1_codes = [
            keep.tile([R2, P], U32, name="h1_codes%d" % bt, align_bytes=64) for bt in range(B_TILES)
        ]
        h1_scales = [
            keep.tile([R2, P], U8, name="h1_scales%d" % bt, align_bytes=64) for bt in range(B_TILES)
        ]

        def transpose_words(k, xt):
            u, h = divmod(k, PAIRS)
            bt, c = divmod(u, PASSES)
            x_words = x_sb[bt][:].bitcast(F32).rearrange("b (i w) -> b w i", w=WORDS)
            for j in range(PACK):
                nc.tensor.transpose(xt[:, j, :], x_words[:, (PACK * c + j) * PAIRS + h, :], ident[:])

        def empty_transposes(k, xt):
            xT_out = xT[k][:].rearrange("i (b j) -> i b j", j=PACK)
            if k in (1, 4, 6):
                nc.scalar.copy(out=xT_out, in_=xt[:].rearrange("i j b -> i b j"))
            else:
                nc.vector.tensor_copy(out=xT_out, in_=xt[:].rearrange("i j b -> i b j"))

        def multiply_slab(s):
            u, bh = divmod(s, HALVES)
            transposing = s + AHEAD < GROUPS_T
            last = s == SLABS - 1
            if transposing:
                xt = xt_banks.tile([I0, PACK, P], F32, tag="xt")
            h0_out = h0_bf[s][:].rearrange("p (b h n) -> p h b n", b=HALF, h=PAIRS)
            if not last:
                h0 = h0_banks.tile([P, HALF, PAIRS, 2, PACK], BF16, tag="h0")
            for h in range(PAIRS):
                x_cols = xT[u * PAIRS + h][:].bitcast(BF16).rearrange(
                    "i (b j e) -> i b e j", j=PACK, e=2
                )
                if last:
                    h0_pair = h0_banks.tile([P, HALF, 2, PACK], BF16, tag="h0")
                nc.tensor.matmul(
                    out=h0_pair[:] if last else h0[:, :, h, :, :],
                    lhsT=core0_p[:],
                    rhs=x_cols[:, bh * HALF : (bh + 1) * HALF, :, :],
                    start=True,
                    stop=True,
                )
                if last:
                    h0_in = h0_pair[:].rearrange("p b e j -> p b (e j)")
                    if h == 0:
                        nc.scalar.copy(out=h0_out[:, h, :, :], in_=h0_in)
                    else:
                        nc.vector.tensor_copy(out=h0_out[:, h, :, :], in_=h0_in)
            if transposing:
                transpose_words(s + AHEAD, xt)
            if not last:
                nc.scalar.copy(out=h0_bf[s][:], in_=h0[:].rearrange("p b h e j -> p (b h e j)"))
            if transposing:
                empty_transposes(s + AHEAD, xt)

        def quantise_slab(s):
            u, bh = divmod(s, HALVES)
            cols = slice(bh * SLAB_COLS, (bh + 1) * SLAB_COLS)
            nc.vector.quantize_mx(
                out=h0_codes[u][:, cols].bitcast(FP8X4), scales=h0_scales[u][:, cols], in_=h0_bf[s][:]
            )

        w1_codes = keep.tile([P, PASSES, R2], U32, align_bytes=64)
        w1_scales = keep.tile([P, PASSES, R2], U8, align_bytes=64)

        w1_bf = keep.tile([P, PASSES, R2, PACK], BF16, align_bytes=64)

        def interleave_core1(c):
            core1_passes = core1_sb[:].rearrange("p (c j k) -> p c k j", c=PASSES, j=PACK)
            nc.vector.tensor_copy(out=w1_bf[:, c, :, :], in_=core1_passes[:, c, :, :])

        def quantise_core1():
            nc.vector.quantize_mx(
                out=w1_codes[:].rearrange("p c k -> p (c k)").bitcast(FP8X4),
                scales=w1_scales[:].rearrange("p c k -> p (c k)"),
                in_=w1_bf[:].rearrange("p c k j -> p (c k j)"),
            )

        h1_bf = [
            keep.tile([R2, COLS], BF16, name="h1_bf%d" % bt, align_bytes=64) for bt in range(B_TILES)
        ]

        def multiply_core1(h1, bt, bh, c):
            u = bt * PASSES + c
            cols = slice(bh * SLAB_COLS, (bh + 1) * SLAB_COLS)
            nc.tensor.matmul_mx(
                out=h1,
                lhsT=w1_codes[:, c, :].bitcast(FP8X4),
                lhsT_scale=w1_scales[:, c, :],
                rhs=h0_codes[u][:, cols].bitcast(FP8X4),
                rhs_scale=h0_scales[u][:, cols],
                start=(c == 0),
                stop=(c == PASSES - 1),
            )

        def quantise_h1(bt, vectors):
            cols = slice(vectors.start * I2, vectors.stop * I2)
            nc.vector.quantize_mx(
                out=h1_codes[bt][:, vectors].bitcast(FP8X4),
                scales=h1_scales[bt][:, vectors],
                in_=h1_bf[bt][:, cols],
            )

        def third_contraction(bt, acc):
            nc.tensor.matmul_mx(
                out=acc[:],
                lhsT=h1_codes[bt][:].bitcast(FP8X4),
                lhsT_scale=h1_scales[bt][:],
                rhs=w2_codes[:].bitcast(FP8X4),
                rhs_scale=w2_scales[:],
                start=True,
                stop=True,
            )

        out_sb = [keep.tile([P, O2], F32, name="out_sb%d" % bt) for bt in range(B_TILES)]

        def store(bt):
            nc.sync.dma_start(
                out=out.rearrange("b x y o -> b (x y o)")[bt * P : (bt + 1) * P, :], in_=out_sb[bt][:]
            )

        ident = keep.tile([P, P], F32)
        make_identity(nc, ident[:])
        core0_p = keep.tile([I0, P], BF16)
        nc.vector.tensor_copy(out=partitions_split(core0_p[:]), in_=ranks_by_partition(core0_sb[:]))

        w2_codes = keep.tile([R2, O2], U32, align_bytes=64)
        w2_scales = keep.tile([R2, O2], U8, align_bytes=64)

        for k in range(AHEAD):
            xt = xt_banks.tile([I0, PACK, P], F32, tag="xt")
            transpose_words(k, xt)
            empty_transposes(k, xt)
        for s in range(SLABS):
            multiply_slab(s)
            if s == SLABS - 1:
                quantise_slab(s - 1)
            if s != SLABS - 2:
                quantise_slab(s)
            if s in (2, 3):
                interleave_core1(s - 2)
            elif s == 4:
                quantise_core1()
                nc.vector.quantize_mx(
                    out=w2_codes[:].bitcast(FP8X4), scales=w2_scales[:], in_=core2_sb[:]
                )

        h1_first = h1_banks.tile([R2, COLS], F32, tag="h1")
        for bh in range(HALVES):
            for c in range(PASSES):
                multiply_core1(h1_first[:, bh * SLAB_COLS : (bh + 1) * SLAB_COLS], 0, bh, c)
        h1_last = [xt_banks.tile([R2, SLAB_COLS], F32, tag="xt", name="h1_last%d" % bh) for bh in range(HALVES)]
        for c in range(PASSES):
            for bh in range(HALVES):
                multiply_core1(h1_last[bh][:], 1, bh, c)
        nc.scalar.copy(out=h1_bf[0][:], in_=h1_first[:])
        nc.vector.tensor_copy(out=h1_bf[1][:, 0:SLAB_COLS], in_=h1_last[0][:])
        quantise_h1(0, slice(0, P))
        nc.scalar.copy(out=h1_bf[1][:, SLAB_COLS:COLS], in_=h1_last[1][:])
        for bh in range(HALVES):
            quantise_h1(1, slice(bh * HALF, (bh + 1) * HALF))
        acc_first = out_banks.tile([P, O2], F32, tag="acc")
        third_contraction(0, acc_first)
        acc_last = xt_banks.tile([P, O2], F32, tag="xt")
        third_contraction(1, acc_last)
        nc.scalar.copy(out=out_sb[0][:], in_=acc_first[:])
        store(0)
        nc.vector.tensor_copy(out=out_sb[1][:], in_=acc_last[:])
        store(1)
